import numpy as np
import ml_dtypes


def mxq(x, axis, fmt="e4m3"):
    dtype, down = {"e4m3": (ml_dtypes.float8_e4m3fn, 7), "e5m2": (ml_dtypes.float8_e5m2, 14)}[fmt]
    v = np.moveaxis(np.asarray(x, np.float32).astype(ml_dtypes.bfloat16).astype(np.float64), axis, -1)
    blocks = v.reshape(v.shape[:-1] + (-1, 32))
    amax = np.abs(blocks).max(-1, keepdims=True)
    byte = np.maximum(np.where(amax > 0, np.frexp(amax)[1] - 1 + 127, 0) - down, 1)
    scale = np.exp2(byte - 127.0)
    codes = (blocks / scale).astype(np.float32).astype(dtype).astype(np.float64)
    return np.moveaxis((codes * scale).reshape(v.shape), -1, axis)


WIDE = False


def mx_kscale(k):
    if not WIDE:
        return np.ones(k)
    levels = np.array([10, -10, 5, -5, 0])
    if k % 512:
        return np.exp2(np.random.permutation(np.resize(levels, k // 32))).repeat(32)
    a = np.empty((k // 512, 16))
    for p in range(k // 512):
        a[p, :8] = np.random.permutation(np.resize(levels, 8))
        for g in range(8):
            far = levels[np.abs(levels - a[p, g]) >= 10]
            a[p, g + 8] = far[np.random.randint(len(far))]
    return np.exp2(a.ravel()).repeat(32)


BF16 = ml_dtypes.bfloat16


def bf(x):
    return np.asarray(x, np.float32).astype(BF16)


def f64(x):
    return np.asarray(x).astype(np.float64)


E2M1 = np.array([0.0, 0.5, 1.0, 1.5, 2.0, 3.0, 4.0, 6.0, -0.0, -0.5, -1.0, -1.5, -2.0, -3.0, -4.0, -6.0])


def pack_weight(w, fmt):
    k, n = w.shape
    w = f64(bf(w)).reshape(k // 32, 32, n)
    amax = np.abs(w).max(1)
    if fmt == "e4m3":
        byte = np.frexp(amax)[1] - 1 + 127 - 7
    else:
        mant, ex = np.frexp(amax / 6.0)
        byte = np.where(mant > 0.5, ex, ex - 1) + 127
    byte = np.clip(np.where(amax > 0, byte, 1), 1, 254)
    scaled = (w * np.exp2(127.0 - byte)[:, None, :]).reshape(k, n).astype(np.float32)
    by_word = np.ascontiguousarray(scaled.reshape(k // 512, 128, 4, n).transpose(0, 1, 3, 2))
    if fmt == "e4m3":
        words = by_word.astype(ml_dtypes.float8_e4m3fn).view(np.uint8)
    else:
        c = by_word.astype(ml_dtypes.float4_e2m1fn).view(np.uint8) & 0xF
        words = c[..., 0::2] | (c[..., 1::2] << 4)
    return np.ascontiguousarray(words), np.ascontiguousarray(byte.astype(np.uint8).reshape(k // 512, 16, n))


def unpack_weight(words, scales, fmt):
    g, p, n, _ = words.shape
    if fmt == "e4m3":
        vals = np.ascontiguousarray(words).view(ml_dtypes.float8_e4m3fn).astype(np.float64)
    else:
        nib = np.empty((g, p, n, 4), np.uint8)
        nib[..., 0::2] = words & 0xF
        nib[..., 1::2] = words >> 4
        vals = E2M1[nib]
    vals = vals * np.repeat(np.exp2(scales.astype(np.float64) - 127.0), 8, axis=1)[..., None]
    return vals.transpose(0, 1, 3, 2).reshape(g * 512, n)


B, S, D, F, F2 = 4, 1024, 512, 512, 1024
EPS = 1e-6
D2 = 2 * D


def draw0():
    n = np.random.standard_normal
    s, t = mx_kscale(F), mx_kscale(D2)
    tr, ti = t[:D], t[D:]
    wd = 1.5 / np.sqrt(F)
    h_r = bf(n((B, S, F)) * 0.6 * s)
    h_i = bf(n((B, S, F)) * 0.6 * s)
    w2r_words, w2r_scales = pack_weight(n((F, D)) * wd / s[:, None] * tr, "e4m3")
    b2r = bf(n(D) * 0.2 * tr)
    w2i_words, w2i_scales = pack_weight(n((F, D)) * wd / s[:, None] * ti, "e4m3")
    b2i = bf(n(D) * 0.2 * ti)
    We_words, We_scales = pack_weight(n((D2, D)) / np.sqrt(D2) / t[:, None], "e4m3")
    return {'h_r': h_r, 'h_i': h_i,
            'w2r_words': w2r_words, 'w2r_scales': w2r_scales, 'b2r': b2r,
            'w2i_words': w2i_words, 'w2i_scales': w2i_scales, 'b2i': b2i,
            'We_words': We_words, 'We_scales': We_scales, 'be': bf(n(D) * 0.2),
            'g_rms': bf(1.0 + 0.1 * n(D))}


def core(h_r, h_i, w2r_words, w2r_scales, b2r, w2i_words, w2i_scales, b2i, We_words, We_scales, be, g_rms):
    rp = (mxq(f64(h_r), 2, 'e4m3') @ unpack_weight(w2r_words, w2r_scales, 'e4m3')) + f64(b2r)
    ip = (mxq(f64(h_i), 2, 'e4m3') @ unpack_weight(w2i_words, w2i_scales, 'e4m3')) + f64(b2i)
    cat = np.concatenate([rp, ip], axis=-1)
    wave = (mxq(cat, 2, 'e4m3') @ unpack_weight(We_words, We_scales, 'e4m3')) + f64(be)
    return wave * (1.0 / np.sqrt(np.mean(wave * wave, axis=-1, keepdims=True) + EPS)) * f64(g_rms)


def e4m3fn_bytes(y):
    return np.clip(np.asarray(y, np.float64), -448.0, 448.0).astype(np.float32).astype(ml_dtypes.float8_e4m3fn).view(np.uint8)


def e4m3fn_values(b):
    return np.asarray(b, np.uint8).view(ml_dtypes.float8_e4m3fn).astype(np.float64)


def setup_inputs():
    d = draw0()
    x0 = np.asarray(d['h_r']).astype(np.float64)
    s = (np.max(np.abs(x0), axis=(0, 1), keepdims=True) / 448.0).astype(np.float32)
    out = {}
    for k, v in d.items():
        if k == 'h_r':
            out['h_r_bytes'] = e4m3fn_bytes(x0 / s.astype(np.float64))
            out['h_r_scale'] = s
        else:
            out[k] = v
    return out


def reference(h_r_bytes, h_r_scale, h_i, w2r_words, w2r_scales, b2r, w2i_words, w2i_scales, b2i, We_words, We_scales, be, g_rms):
    return core(e4m3fn_values(h_r_bytes) * h_r_scale.astype(np.float64), h_i, w2r_words, w2r_scales, b2r, w2i_words, w2i_scales, b2i, We_words, We_scales, be, g_rms)

@@ -1,0 +1,367 @@
+from contextlib import ExitStack
+
+import concourse.mybir as mybir
+from concourse.masks import make_identity
+
+FLOPS = 2 * 4096 * 512 * 512 * 2 + 2 * 4096 * 1024 * 512
+EPS = 1e-6
+
+F32 = mybir.dt.float32
+BF16 = mybir.dt.bfloat16
+U32 = mybir.dt.uint32
+I32 = mybir.dt.int32
+U8 = mybir.dt.uint8
+FP8 = mybir.dt.float8_e4m3fn
+FP8X4 = mybir.dt.float8_e4m3fn_x4
+ACT = mybir.ActivationFunctionType
+ALU = mybir.AluOpType
+
+P = 128
+T = 4
+K = 512
+D = 512
+NB = 512
+J = NB // P
+BLOCKS = 8
+REST = 96
+
+STEP = [
+    (1, "copy_in", (1, 0)),
+    (5, "finish", (3,)),
+    (2, "project_i", (0,)),
+    (4, "square", (1,)),
+    (1, "product", (1,)),
+    (1, "turn_in", (0, 1)),
+    (2, "bias_r", (1,)),
+    (3, "combine", (2,)),
+    (2, "bias_i", (2,)),
+    (5, "inv_rms_last", (2,)),
+    (3, "combine", (0,)),
+    (1, "copy_in", (0, 0)),
+    (5, "finish", (2,)),
+    (4, "inv_rms_last", (1,)),
+    (1, "quantise_h", (1,)),
+    (1, "project_i", (1,)),
+    (4, "turn_out", (2,)),
+    (3, "bias_e", (1,)),
+    (3, "bias_e_last", (1,)),
+    (0, "turn_in", (1, 1)),
+    (4, "square", (0,)),
+    (2, "bias_r", (2,)),
+    (1, "project_i", (3,)),
+    (0, "product", (0,)),
+    (4, "inv_rms", (0,)),
+    (4, "finish", (1,)),
+    (4, "inv_rms_last", (0,)),
+    (4, "finish", (0,)),
+    (2, "bias_r", (0,)),
+    (3, "bias_e", (3,)),
+    (2, "bias_i", (0,)),
+    (2, "interleave_rest", ()),
+    (2, "interleave", ()),
+    (1, "copy_in", (0, 1)),
+    (1, "quantise_h", (0,)),
+    (1, "project_r", (3,)),
+    (0, "turn_in", (1, 0)),
+    (4, "square", (3,)),
+    (4, "inv_rms_last", (3,)),
+    (2, "quantise_cat", (1,)),
+    (3, "bias_e", (2,)),
+    (1, "bias_i", (1,)),
+    (3, "bias_e", (0,)),
+    (1, "bias_i", (3,)),
+    (4, "square", (2,)),
+    (0, "copy_in", (1, 1)),
+    (2, "quantise_cat", (0,)),
+    (4, "inv_rms", (1,)),
+    (3, "bias_e_last", (3,)),
+    (3, "turn_out", (1,)),
+    (1, "project_r", (1,)),
+    (1, "project_i", (2,)),
+    (0, "turn_in", (0, 0)),
+    (2, "combine", (1,)),
+    (3, "turn_out", (0,)),
+    (1, "project_r", (2,)),
+    (1, "project_r", (0,)),
+    (2, "combine", (3,)),
+    (3, "turn_out", (3,)),
+    (1, "bias_r", (3,)),
+]
+LAG = 5
+
+
+def tile_wavenetworklm_pb_t_w8_kernel(
+    tc, h_r_bytes, h_r_scale, h_i, w2r_words, w2r_scales, b2r, w2i_words, w2i_scales, b2i, We_words, We_scales, be, g_rms, out
+):
+    nc = tc.nc
+    split = "b (h p j) k -> (b h) p j k"
+    hr_src = h_r_bytes.rearrange(split, h=2, p=P, j=J)
+    hi_src = h_i.rearrange(split, h=2, p=P, j=J)
+    out_dst = out.rearrange(split, h=2, p=P, j=J)
+
+    with ExitStack() as ctx:
+        keep = ctx.enter_context(tc.tile_pool(name="keep", bufs=1))
+        loads = ctx.enter_context(tc.tile_pool(name="loads", bufs=BLOCKS))
+        work = ctx.enter_context(tc.tile_pool(name="work", bufs=3))
+        psum_t = ctx.enter_context(tc.psum_pool(name="psum_t", bufs=2))
+        psum_m = ctx.enter_context(tc.psum_pool(name="psum_m", bufs=3))
+        psum_o = ctx.enter_context(tc.psum_pool(name="psum_o", bufs=3))
+        ctx.enter_context(tc.manual_schedule())
+
+        ident = keep.tile([P, P], F32, name="ident")
+        one_col = keep.tile([P, 1], F32, name="one_col")
+        warm = keep.tile([P, 1], F32, name="warm")
+        ones = keep.tile([P, P], BF16, name="ones")
+        ident_b = keep.tile([P, T], BF16, name="ident_b")
+        rows = keep.tile([P, D], BF16, name="rows")
+        rows4 = keep.tile([P, P], BF16, name="rows4")
+        scl2 = keep.tile([P, D], U8, name="scl2", align_bytes=64)
+        scle = keep.tile([P, D], U8, name="scle", align_bytes=64)
+        scl2p = keep.tile([P, D], U8, name="scl2p", align_bytes=64)
+        w2 = [keep.tile([P, D], U32, name=f"w2_{s}", align_bytes=64) for s in range(2)]
+        w2p = [keep.tile([P, D], U32, name=f"w2p_{s}", align_bytes=64) for s in range(2)]
+        we = keep.tile([P, 2, D], U32, name="we", align_bytes=64)
+        hscale = keep.tile([P, 2, K], F32, name="hscale")
+        bcol = [keep.tile([P, T], BF16, name=f"bcol_{s}") for s in range(2)]
+        be_col = keep.tile([P, T], F32, name="be_col")
+        g_t = keep.tile([P, D], F32, name="g_t")
+
+        nc.gpsimd.memset(scl2[:].bitcast(I32), 0)
+        nc.gpsimd.memset(one_col[:], 1.0)
+        nc.gpsimd.memset(rows[:], 0.0)
+        nc.gpsimd.memset(rows4[:], 0.0)
+        make_identity(nc, ident[:])
+        nc.gpsimd.tensor_copy(out=ident_b[:], in_=ident[:, 0:T])
+        nc.gpsimd.memset(scle[:].bitcast(I32), 0)
+        nc.gpsimd.memset(ones[:], 1.0)
+
+        hb = [loads.tile([P, J, K], U8, name="hb", align_bytes=64) for i in range(BLOCKS)]
+        hi = [loads.tile([P, J, K], BF16, name="hi", align_bytes=64) for i in range(BLOCKS)]
+        words = [w2r_words, w2i_words]
+        scales = [w2r_scales, w2i_scales]
+
+        nc.scalar.dma_start(out=hscale[:, 0, :], in_=h_r_scale.rearrange("a b k -> (a b k)").partition_broadcast(P))
+        nc.scalar.dma_start(out=bcol[1][:], in_=b2i.rearrange("(p t) -> p t", t=T))
+        nc.scalar.dma_start(out=bcol[0][:], in_=b2r.rearrange("(p t) -> p t", t=T))
+        nc.scalar.dma_start(out=rows4[0:T, :], in_=be.rearrange("(c m) -> c m", c=T))
+        nc.scalar.dma_start(out=rows[0:1, :], in_=g_rms.unsqueeze(0))
+
+        def load_words(s):
+            nc.sync.dma_start(out=w2[s][:].bitcast(I32), in_=words[s][0].rearrange("p n t -> p (n t)").bitcast(I32))
+
+        def load_scales(s):
+            for q in range(4):
+                nc.sync.dma_start(
+                    out=scl2[32 * q + 4 * s : 32 * q + 4 * s + 4, :].bitcast(I32),
+                    in_=scales[s][0, 4 * q : 4 * q + 4, :].bitcast(I32),
+                )
+
+        load_words(1)
+        nc.sync.dma_start(out=hb[0][:], in_=hr_src[0])
+        load_words(0)
+        nc.sync.dma_start(out=hi[0][:], in_=hi_src[0])
+        load_scales(1)
+        load_scales(0)
+        nc.sync.dma_start(out=hb[1][:], in_=hr_src[1])
+        nc.sync.dma_start(out=hi[1][:], in_=hi_src[1])
+        nc.sync.dma_start(
+            out=we[:].rearrange("p g n -> p g n").bitcast(I32),
+            in_=We_words.rearrange("g p n t -> p g (n t)").bitcast(I32),
+        )
+        for q in range(4):
+            nc.sync.dma_start(
+                out=scle[32 * q : 32 * q + 8, :].bitcast(I32), in_=We_scales[:, 4 * q : 4 * q + 4, :].bitcast(I32)
+            )
+        for i in range(2, BLOCKS):
+            nc.sync.dma_start(out=hb[i][:], in_=hr_src[i])
+            nc.sync.dma_start(out=hi[i][:], in_=hi_src[i])
+
+        nc.scalar.activation(out=warm[:], in_=one_col[:], func=ACT.Abs_reciprocal_sqrt)
+        nc.scalar.copy(out=hscale[:, 1, :], in_=hscale[:, 0, :])
+
+        hr, hq, hs, y, cq, cs = {}, {}, {}, {}, {}, {}
+        grouped, catg, wt, turned, res, rstd, xt, ps = {}, {}, {}, {}, {}, {}, {}, {}
+
+        def first(store, key, make):
+            if key not in store:
+                store[key] = make()
+            return store[key]
+
+        def product(i, half):
+            t = first(hr, i, lambda: work.tile([P, J, K], BF16, name="hr", align_bytes=64))
+            pair = slice(2 * half, 2 * half + 2)
+            nc.vector.tensor_tensor(out=t[:, pair, :], in0=hb[i][:, pair, :].bitcast(FP8), in1=hscale[:], op=ALU.mult)
+
+        def turn_in(i, s, half):
+            src = hr[i] if s == 0 else hi[i]
+            xt[i, s, half] = psum_t.tile([P, 2, 2, P], F32, name="xt")
+            for jj in range(2):
+                pairs = src[:, 2 * half + jj, :].bitcast(F32)
+                for u in range(2):
+                    nc.tensor.transpose(xt[i, s, half][:, jj, u, :], pairs[:, u : K // 2 : 2], ident[:])
+
+        def copy_in(i, s, half):
+            t = first(grouped, (i, s), lambda: work.tile([P, NB, T], BF16, name=f"grouped{s}", align_bytes=64))
+            dst = t[:].rearrange("p n t -> p (n t)").bitcast(F32)
+            nc.scalar.copy(
+                out=dst[:, half * NB : (half + 1) * NB].rearrange("p (j r u) -> p j r u", j=2, u=2),
+                in_=xt[i, s, half][:].rearrange("p j u r -> p j r u"),
+            )
+
+        def quantise_h(i, s):
+            hq[i, s] = work.tile([P, NB], U32, name=f"hq{s}", align_bytes=64)
+            hs[i, s] = work.tile([P, NB], U8, name=f"hs{s}", align_bytes=64)
+            nc.vector.quantize_mx(
+                out=hq[i, s][:].bitcast(FP8X4), scales=hs[i, s][:], in_=grouped[i, s][:].rearrange("p n t -> p (n t)")
+            )
+
+        def project(out_ap, i, s, t, toks):
+            cols = slice(P * t, P * (t + 1))
+            nc.tensor.matmul_mx(
+                out=out_ap,
+                lhsT=w2p[s][:, cols].bitcast(FP8X4),
+                lhsT_scale=scl2p[4 * s : P, cols],
+                rhs=hq[i, s][:, toks].bitcast(FP8X4),
+                rhs_scale=hs[i, s][:, toks],
+                start=True,
+                stop=True,
+            )
+
+        def project_i(i, j):
+            ps[i, "i", j] = psum_m.tile([P, T, P], F32, name="ps")
+            for t in range(T):
+                project(ps[i, "i", j][:, t, :], i, 1, t, slice(P * j, P * (j + 1)))
+
+        def bias_i(i, j):
+            t = first(catg, (i, 1), lambda: work.tile([P, NB, T], BF16, name="catg1", align_bytes=64))
+            nc.vector.tensor_tensor(
+                out=t[:, P * j : P * (j + 1), :],
+                in0=ps[i, "i", j][:].rearrange("p t n -> p n t"),
+                in1=bcol[1][:].unsqueeze(1).to_broadcast([P, P, T]),
+                op=ALU.add,
+            )
+
+        def project_r(i, t):
+            ps[i, "r", t] = psum_m.tile([P, NB], F32, name="ps")
+            project(ps[i, "r", t][:], i, 0, t, slice(0, NB))
+
+        def bias_r(i, t):
+            yt = first(y, i, lambda: work.tile([P, T, NB], BF16, name="y", align_bytes=64))
+            nc.scalar.activation(out=yt[:, t, :], in_=ps[i, "r", t][:], func=ACT.Identity, bias=bcol[0][:, t : t + 1], scale=1.0)
+
+        def interleave_views(i, toks):
+            t = first(catg, (i, 0), lambda: work.tile([P, NB, T], BF16, name="catg0", align_bytes=64))
+            return (
+                t[:, toks, :].rearrange("p (c i) t -> p c t i", i=4),
+                y[i][:, :, toks].rearrange("p t (c i) -> p c t i", i=4),
+            )
+
+        def interleave(i):
+            dst, src = interleave_views(i, slice(0, NB - REST))
+            nc.vector.tensor_copy(out=dst, in_=src)
+
+        def interleave_rest(i):
+            dst, src = interleave_views(i, slice(NB - REST, NB))
+            nc.scalar.copy(out=dst, in_=src)
+
+        def quantise_cat(i, s):
+            cq[i, s] = work.tile([P, NB], U32, name=f"cq{s}", align_bytes=64)
+            cs[i, s] = work.tile([P, NB], U8, name=f"cs{s}", align_bytes=64)
+            nc.vector.quantize_mx(
+                out=cq[i, s][:].bitcast(FP8X4), scales=cs[i, s][:], in_=catg[i, s][:].rearrange("p n t -> p (n t)")
+            )
+
+        def combine(i, c):
+            ps[i, "e", c] = psum_m.tile([P, NB], F32, name="ps")
+            cols = slice(P * c, P * (c + 1))
+            for s in range(2):
+                nc.tensor.matmul_mx(
+                    out=ps[i, "e", c][:],
+                    lhsT=we[:, s, cols].bitcast(FP8X4),
+                    lhsT_scale=scle[4 * s : P, cols],
+                    rhs=cq[i, s][:].bitcast(FP8X4),
+                    rhs_scale=cs[i, s][:],
+                    start=(s == 0),
+                    stop=(s == 1),
+                )
+
+        def wave_tile(i):
+            return first(wt, i, lambda: work.tile([P, T, NB], F32, name="wt"))
+
+        def bias_e(i, c):
+            if i < BLOCKS - 1 or c % 2 == 0:
+                nc.scalar.activation(
+                    out=wave_tile(i)[:, c, :], in_=ps[i, "e", c][:], func=ACT.Identity, bias=be_col[:, c : c + 1], scale=1.0
+                )
+
+        def bias_e_last(i, c):
+            if i == BLOCKS - 1:
+                nc.vector.tensor_scalar(
+                    out=wave_tile(i)[:, c, :], in0=ps[i, "e", c][:], scalar1=be_col[:, c : c + 1], scalar2=None, op0=ALU.add
+                )
+
+        def turn_out(i, j):
+            turned[i, j] = psum_o.tile([P, T, P], F32, name="turned")
+            for c in range(T):
+                nc.tensor.transpose(turned[i, j][:, c, :], wt[i][:, c, P * j : P * (j + 1)], ident[:])
+
+        def square(i, j):
+            t = first(rstd, i, lambda: work.tile([P, 2 * J], F32, name="rstd"))
+            junk = work.tile([P, D], BF16, name="junk")
+            nc.scalar.activation(
+                out=junk[:], in_=turned[i, j][:].rearrange("p c m -> p (c m)"), func=ACT.Square, accum_out=t[:, j : j + 1]
+            )
+
+        def inv_sqrt(i, a, b):
+            nc.scalar.activation(
+                out=rstd[i][:, J + a : J + b], in_=rstd[i][:, a:b], func=ACT.Abs_reciprocal_sqrt, scale=1.0 / D, bias=EPS
+            )
+
+        def inv_rms(i, half):
+            if i < BLOCKS - 1:
+                inv_sqrt(i, 2 * half, 2 * half + 2)
+
+        def inv_rms_last(i, j):
+            if i == BLOCKS - 1:
+                inv_sqrt(i, j, j + 1)
+
+        def finish(i, j):
+            t = first(res, i, lambda: work.tile([P, J, D], F32, name="res"))
+            nc.vector.scalar_tensor_tensor(
+                out=t[:, j, :],
+                in0=turned[i, j][:].rearrange("p c m -> p (c m)"),
+                scalar=rstd[i][:, J + j : J + j + 1],
+                in1=g_t[:],
+                op0=ALU.mult,
+                op1=ALU.mult,
+            )
+            nc.sync.dma_start(out=out_dst[i][:, j, :], in_=t[:, j, :])
+
+        pieces = {
+            "product": product, "turn_in": turn_in, "copy_in": copy_in, "quantise_h": quantise_h, "project_i": project_i,
+            "bias_i": bias_i, "project_r": project_r, "bias_r": bias_r, "interleave": interleave,
+            "interleave_rest": interleave_rest, "quantise_cat": quantise_cat, "combine": combine, "bias_e": bias_e,
+            "bias_e_last": bias_e_last, "turn_out": turn_out, "square": square, "inv_rms": inv_rms,
+            "inv_rms_last": inv_rms_last, "finish": finish,
+        }
+
+        for n in (1, 0):
+            nc.vector.tensor_copy(
+                out=w2p[n][:].bitcast(I32).rearrange("p (t m) -> p m t", t=T),
+                in_=w2[n][:].bitcast(I32).rearrange("p (m t) -> p m t", t=T),
+            )
+
+        for step in range(BLOCKS + LAG):
+            for lag, piece, args in STEP:
+                if 0 <= step - lag < BLOCKS:
+                    pieces[piece](step - lag, *args)
+            if step == 0:
+                nc.vector.tensor_copy(
+                    out=scl2p[:].rearrange("p (t m) -> p m t", t=T), in_=scl2[:].rearrange("p (m t) -> p m t", t=T)
+                )
+                be_ps = psum_m.tile([P, T], F32, name="ps")
+                nc.tensor.matmul(be_ps[:], rows4[:], ident_b[:], start=True, stop=True)
+                nc.scalar.copy(out=be_col[:], in_=be_ps[:])
+                g_ps = psum_m.tile([P, D], F32, name="ps")
+                nc.tensor.matmul(g_ps[:], ones[:], rows[:], start=True, stop=True)
+                nc.scalar.copy(out=g_t[:], in_=g_ps[:])

@@ -23,69 +23,69 @@ D = 512
 NB = 512
 J = NB // P
 BLOCKS = 8
-REST = 96
+REST = 64
 
 STEP = [
-    (1, "copy_in", (1, 0)),
-    (5, "finish", (3,)),
+    (3, "bias_i", (2,)),
+    (5, "inv_rms_last", (3,)),
+    (5, "turn_out", (2,)),
+    (5, "square", (2,)),
     (2, "project_i", (0,)),
-    (4, "square", (1,)),
+    (4, "bias_e_last", (3,)),
+    (5, "inv_rms", (1,)),
+    (2, "project_i", (1,)),
+    (3, "interleave", ()),
+    (3, "interleave_rest", ()),
+    (2, "project_r", (2,)),
+    (2, "bias_r", (2,)),
+    (5, "finish", (0,)),
+    (5, "finish", (1,)),
     (1, "product", (1,)),
     (1, "turn_in", (0, 1)),
-    (2, "bias_r", (1,)),
-    (3, "combine", (2,)),
-    (2, "bias_i", (2,)),
-    (5, "inv_rms_last", (2,)),
-    (3, "combine", (0,)),
-    (1, "copy_in", (0, 0)),
-    (5, "finish", (2,)),
-    (4, "inv_rms_last", (1,)),
-    (1, "quantise_h", (1,)),
-    (1, "project_i", (1,)),
-    (4, "turn_out", (2,)),
-    (3, "bias_e", (1,)),
-    (3, "bias_e_last", (1,)),
-    (0, "turn_in", (1, 1)),
-    (4, "square", (0,)),
-    (2, "bias_r", (2,)),
-    (1, "project_i", (3,)),
-    (0, "product", (0,)),
-    (4, "inv_rms", (0,)),
-    (4, "finish", (1,)),
-    (4, "inv_rms_last", (0,)),
-    (4, "finish", (0,)),
-    (2, "bias_r", (0,)),
-    (3, "bias_e", (3,)),
-    (2, "bias_i", (0,)),
-    (2, "interleave_rest", ()),
-    (2, "interleave", ()),
     (1, "copy_in", (0, 1)),
+    (0, "turn_in", (1, 0)),
+    (0, "copy_in", (1, 0)),
+    (3, "quantise_cat", (1,)),
+    (4, "bias_e_last", (1,)),
+    (4, "turn_out", (0,)),
+    (2, "project_r", (0,)),
+    (2, "bias_r", (0,)),
+    (2, "project_r", (1,)),
+    (2, "bias_r", (1,)),
+    (4, "square", (0,)),
+    (4, "inv_rms_last", (0,)),
+    (2, "project_i", (3,)),
+    (1, "quantise_h", (1,)),
+    (5, "inv_rms_last", (2,)),
+    (4, "turn_out", (1,)),
+    (4, "square", (1,)),
+    (2, "bias_i", (0,)),
+    (0, "turn_in", (1, 1)),
+    (0, "copy_in", (1, 1)),
+    (2, "bias_i", (1,)),
+    (2, "project_i", (2,)),
+    (4, "inv_rms", (0,)),
+    (5, "finish", (3,)),
+    (3, "quantise_cat", (0,)),
+    (3, "combine", (0,)),
+    (3, "bias_e", (0,)),
+    (3, "combine", (3,)),
+    (3, "bias_e", (3,)),
+    (4, "inv_rms_last", (1,)),
+    (3, "combine", (2,)),
+    (0, "product", (0,)),
+    (3, "bias_e", (2,)),
+    (3, "combine", (1,)),
+    (5, "finish", (2,)),
+    (3, "bias_e", (1,)),
+    (2, "bias_i", (3,)),
     (1, "quantise_h", (0,)),
     (1, "project_r", (3,)),
-    (0, "turn_in", (1, 0)),
-    (4, "square", (3,)),
-    (4, "inv_rms_last", (3,)),
-    (2, "quantise_cat", (1,)),
-    (3, "bias_e", (2,)),
-    (1, "bias_i", (1,)),
-    (3, "bias_e", (0,)),
-    (1, "bias_i", (3,)),
-    (4, "square", (2,)),
-    (0, "copy_in", (1, 1)),
-    (2, "quantise_cat", (0,)),
-    (4, "inv_rms", (1,)),
-    (3, "bias_e_last", (3,)),
-    (3, "turn_out", (1,)),
-    (1, "project_r", (1,)),
-    (1, "project_i", (2,)),
-    (0, "turn_in", (0, 0)),
-    (2, "combine", (1,)),
-    (3, "turn_out", (0,)),
-    (1, "project_r", (2,)),
-    (1, "project_r", (0,)),
-    (2, "combine", (3,)),
-    (3, "turn_out", (3,)),
     (1, "bias_r", (3,)),
+    (0, "turn_in", (0, 0)),
+    (0, "copy_in", (0, 0)),
+    (4, "turn_out", (3,)),
+    (4, "square", (3,)),
 ]
 LAG = 5
 
@@ -112,6 +112,8 @@ def tile_wavenetworklm_pb_t_w8_kernel(
         one_col = keep.tile([P, 1], F32, name="one_col")
         warm = keep.tile([P, 1], F32, name="warm")
         ones = keep.tile([P, P], BF16, name="ones")
+        ones_f = keep.tile([P, P], F32, name="ones_f")
+        scale_row = keep.tile([P, K], F32, name="scale_row")
         ident_b = keep.tile([P, T], BF16, name="ident_b")
         rows = keep.tile([P, D], BF16, name="rows")
         rows4 = keep.tile([P, P], BF16, name="rows4")
@@ -126,21 +128,24 @@ def tile_wavenetworklm_pb_t_w8_kernel(
         be_col = keep.tile([P, T], F32, name="be_col")
         g_t = keep.tile([P, D], F32, name="g_t")
 
-        nc.gpsimd.memset(scl2[:].bitcast(I32), 0)
+        nc.vector.memset(scl2[:].bitcast(I32), 0)
+        nc.vector.memset(scle[:].bitcast(I32), 0)
         nc.gpsimd.memset(one_col[:], 1.0)
-        nc.gpsimd.memset(rows[:], 0.0)
-        nc.gpsimd.memset(rows4[:], 0.0)
+        nc.gpsimd.memset(scale_row[:], 0.0)
+        nc.gpsimd.memset(ones_f[:], 1.0)
         make_identity(nc, ident[:])
-        nc.gpsimd.tensor_copy(out=ident_b[:], in_=ident[:, 0:T])
-        nc.gpsimd.memset(scle[:].bitcast(I32), 0)
+        nc.gpsimd.memset(rows4[:], 0.0)
+        nc.gpsimd.memset(rows[:], 0.0)
         nc.gpsimd.memset(ones[:], 1.0)
+        nc.gpsimd.tensor_copy(out=ident_b[:], in_=ident[:, 0:T])
 
         hb = [loads.tile([P, J, K], U8, name="hb", align_bytes=64) for i in range(BLOCKS)]
         hi = [loads.tile([P, J, K], BF16, name="hi", align_bytes=64) for i in range(BLOCKS)]
         words = [w2r_words, w2i_words]
         scales = [w2r_scales, w2i_scales]
 
-        nc.scalar.dma_start(out=hscale[:, 0, :], in_=h_r_scale.rearrange("a b k -> (a b k)").partition_broadcast(P))
+        nc.scalar.dma_start(out=scale_row[0:1, :], in_=h_r_scale.rearrange("a b k -> (a b) k"))
+        nc.scalar.activation(out=warm[:], in_=one_col[:], func=ACT.Abs_reciprocal_sqrt)
         nc.scalar.dma_start(out=bcol[1][:], in_=b2i.rearrange("(p t) -> p t", t=T))
         nc.scalar.dma_start(out=bcol[0][:], in_=b2r.rearrange("(p t) -> p t", t=T))
         nc.scalar.dma_start(out=rows4[0:T, :], in_=be.rearrange("(c m) -> c m", c=T))
@@ -156,10 +161,10 @@ def tile_wavenetworklm_pb_t_w8_kernel(
                     in_=scales[s][0, 4 * q : 4 * q + 4, :].bitcast(I32),
                 )
 
+        nc.sync.dma_start(out=hi[0][:], in_=hi_src[0])
         load_words(1)
         nc.sync.dma_start(out=hb[0][:], in_=hr_src[0])
         load_words(0)
-        nc.sync.dma_start(out=hi[0][:], in_=hi_src[0])
         load_scales(1)
         load_scales(0)
         nc.sync.dma_start(out=hb[1][:], in_=hr_src[1])
@@ -176,9 +181,6 @@ def tile_wavenetworklm_pb_t_w8_kernel(
             nc.sync.dma_start(out=hb[i][:], in_=hr_src[i])
             nc.sync.dma_start(out=hi[i][:], in_=hi_src[i])
 
-        nc.scalar.activation(out=warm[:], in_=one_col[:], func=ACT.Abs_reciprocal_sqrt)
-        nc.scalar.copy(out=hscale[:, 1, :], in_=hscale[:, 0, :])
-
         hr, hq, hs, y, cq, cs = {}, {}, {}, {}, {}, {}
         grouped, catg, wt, turned, res, rstd, xt, ps = {}, {}, {}, {}, {}, {}, {}, {}
 
@@ -190,6 +192,12 @@ def tile_wavenetworklm_pb_t_w8_kernel(
         def product(i, half):
             t = first(hr, i, lambda: work.tile([P, J, K], BF16, name="hr", align_bytes=64))
             pair = slice(2 * half, 2 * half + 2)
+            if i == 0:
+                for j in (2 * half, 2 * half + 1):
+                    nc.vector.tensor_tensor(
+                        out=t[:, j, :], in0=hb[i][:, j, :].bitcast(FP8), in1=hscale[:, 0, :], op=ALU.mult
+                    )
+                return
             nc.vector.tensor_tensor(out=t[:, pair, :], in0=hb[i][:, pair, :].bitcast(FP8), in1=hscale[:], op=ALU.mult)
 
         def turn_in(i, s, half):
@@ -345,17 +353,25 @@ def tile_wavenetworklm_pb_t_w8_kernel(
             "inv_rms_last": inv_rms_last, "finish": finish,
         }
 
-        for n in (1, 0):
+        scale_ps = psum_m.tile([P, K], F32, name="ps")
+        nc.tensor.matmul(scale_ps[:], ones_f[:], scale_row[:], start=True, stop=True)
+
+        def permute_words(n):
             nc.vector.tensor_copy(
                 out=w2p[n][:].bitcast(I32).rearrange("p (t m) -> p m t", t=T),
                 in_=w2[n][:].bitcast(I32).rearrange("p (m t) -> p m t", t=T),
             )
+
+        permute_words(1)
+        nc.vector.tensor_copy(out=hscale[:, 0, :], in_=scale_ps[:])
+        permute_words(0)
 
         for step in range(BLOCKS + LAG):
             for lag, piece, args in STEP:
                 if 0 <= step - lag < BLOCKS:
                     pieces[piece](step - lag, *args)
             if step == 0:
+                nc.scalar.copy(out=hscale[:, 1, :], in_=hscale[:, 0, :])
                 nc.vector.tensor_copy(
                     out=scl2p[:].rearrange("p (t m) -> p m t", t=T), in_=scl2[:].rearrange("p (m t) -> p m t", t=T)
                 )

@@ -23,71 +23,68 @@ D = 512
 NB = 512
 J = NB // P
 BLOCKS = 8
-REST = 64
 
 STEP = [
-    (3, "bias_i", (2,)),
-    (5, "inv_rms_last", (3,)),
-    (5, "turn_out", (2,)),
-    (5, "square", (2,)),
-    (2, "project_i", (0,)),
-    (4, "bias_e_last", (3,)),
-    (5, "inv_rms", (1,)),
-    (2, "project_i", (1,)),
-    (3, "interleave", ()),
-    (3, "interleave_rest", ()),
-    (2, "project_r", (2,)),
-    (2, "bias_r", (2,)),
-    (5, "finish", (0,)),
-    (5, "finish", (1,)),
-    (1, "product", (1,)),
-    (1, "turn_in", (0, 1)),
-    (1, "copy_in", (0, 1)),
-    (0, "turn_in", (1, 0)),
-    (0, "copy_in", (1, 0)),
-    (3, "quantise_cat", (1,)),
-    (4, "bias_e_last", (1,)),
-    (4, "turn_out", (0,)),
-    (2, "project_r", (0,)),
-    (2, "bias_r", (0,)),
-    (2, "project_r", (1,)),
-    (2, "bias_r", (1,)),
-    (4, "square", (0,)),
-    (4, "inv_rms_last", (0,)),
-    (2, "project_i", (3,)),
-    (1, "quantise_h", (1,)),
-    (5, "inv_rms_last", (2,)),
-    (4, "turn_out", (1,)),
-    (4, "square", (1,)),
-    (2, "bias_i", (0,)),
+    (8, "bias_e", (3,)),
+    (10, "finish", (3,)),
+    (7, "interleave", ()),
+    (9, "turn_out", (2,)),
+    (6, "bias_r", (0,)),
+    (6, "project_r", (1,)),
+    (10, "finish", (2,)),
+    (9, "inv_rms_last", (3,)),
+    (6, "project_i", (2,)),
+    (7, "bias_i", (1,)),
+    (1, "copy_in", (1, 1)),
+    (6, "project_i", (0,)),
+    (4, "copy_in", (0, 1)),
+    (4, "turn_in", (0, 0)),
+    (8, "bias_e_vector", (1,)),
+    (6, "bias_r", (1,)),
+    (7, "bias_i", (3,)),
+    (9, "square", (2,)),
+    (4, "copy_in", (0, 0)),
+    (5, "quantise_h", ()),
+    (9, "inv_rms", (1,)),
+    (9, "finish", (0,)),
+    (9, "finish", (1,)),
+    (5, "quantise_h_first", (0,)),
+    (8, "bias_e_vector", (3,)),
+    (8, "turn_out", (0,)),
+    (1, "turn_in", (1, 0)),
+    (8, "square", (0,)),
+    (1, "copy_in", (1, 0)),
+    (8, "inv_rms_last", (0,)),
+    (7, "quantise_cat", ()),
+    (7, "combine", (2,)),
+    (7, "combine", (1,)),
+    (6, "project_i", (1,)),
+    (8, "turn_out", (1,)),
+    (7, "bias_e", (2,)),
+    (6, "project_i", (3,)),
+    (9, "inv_rms_last", (2,)),
+    (5, "project_r", (2,)),
+    (7, "bias_e", (1,)),
+    (7, "combine", (0,)),
+    (8, "square", (1,)),
+    (8, "turn_out", (3,)),
+    (8, "inv_rms", (0,)),
+    (5, "quantise_h_first", (1,)),
+    (5, "project_r", (3,)),
+    (5, "bias_r", (2,)),
+    (7, "combine", (3,)),
+    (1, "product", ()),
+    (7, "bias_e", (0,)),
+    (5, "project_r", (0,)),
+    (8, "inv_rms_last", (1,)),
+    (6, "bias_i", (2,)),
     (0, "turn_in", (1, 1)),
-    (0, "copy_in", (1, 1)),
-    (2, "bias_i", (1,)),
-    (2, "project_i", (2,)),
-    (4, "inv_rms", (0,)),
-    (5, "finish", (3,)),
-    (3, "quantise_cat", (0,)),
-    (3, "combine", (0,)),
-    (3, "bias_e", (0,)),
-    (3, "combine", (3,)),
-    (3, "bias_e", (3,)),
-    (4, "inv_rms_last", (1,)),
-    (3, "combine", (2,)),
-    (0, "product", (0,)),
-    (3, "bias_e", (2,)),
-    (3, "combine", (1,)),
-    (5, "finish", (2,)),
-    (3, "bias_e", (1,)),
-    (2, "bias_i", (3,)),
-    (1, "quantise_h", (0,)),
-    (1, "project_r", (3,)),
-    (1, "bias_r", (3,)),
-    (0, "turn_in", (0, 0)),
-    (0, "copy_in", (0, 0)),
-    (4, "turn_out", (3,)),
-    (4, "square", (3,)),
+    (8, "square", (3,)),
+    (6, "bias_i", (0,)),
+    (3, "turn_in", (0, 1)),
+    (5, "bias_r", (3,)),
 ]
-LAG = 5
+LAG = 10
 
 
 def tile_wavenetworklm_pb_t_w8_kernel(
@@ -123,7 +120,7 @@ def tile_wavenetworklm_pb_t_w8_kernel(
         w2 = [keep.tile([P, D], U32, name=f"w2_{s}", align_bytes=64) for s in range(2)]
         w2p = [keep.tile([P, D], U32, name=f"w2p_{s}", align_bytes=64) for s in range(2)]
         we = keep.tile([P, 2, D], U32, name="we", align_bytes=64)
-        hscale = keep.tile([P, 2, K], F32, name="hscale")
+        hscale = keep.tile([P, J, K], F32, name="hscale")
         bcol = [keep.tile([P, T], BF16, name=f"bcol_{s}") for s in range(2)]
         be_col = keep.tile([P, T], F32, name="be_col")
         g_t = keep.tile([P, D], F32, name="g_t")
@@ -184,21 +181,22 @@ def tile_wavenetworklm_pb_t_w8_kernel(
         hr, hq, hs, y, cq, cs = {}, {}, {}, {}, {}, {}
         grouped, catg, wt, turned, res, rstd, xt, ps = {}, {}, {}, {}, {}, {}, {}, {}
 
+        scale_copies = []
+
         def first(store, key, make):
             if key not in store:
                 store[key] = make()
             return store[key]
 
-        def product(i, half):
-            t = first(hr, i, lambda: work.tile([P, J, K], BF16, name="hr", align_bytes=64))
-            pair = slice(2 * half, 2 * half + 2)
+        def product(i):
+            hr[i] = work.tile([P, J, K], BF16, name="hr", bufs=6, align_bytes=64)
             if i == 0:
-                for j in (2 * half, 2 * half + 1):
+                for j in range(J):
                     nc.vector.tensor_tensor(
-                        out=t[:, j, :], in0=hb[i][:, j, :].bitcast(FP8), in1=hscale[:, 0, :], op=ALU.mult
+                        out=hr[i][:, j, :], in0=hb[i][:, j, :].bitcast(FP8), in1=hscale[:, 0, :], op=ALU.mult
                     )
-                return
-            nc.vector.tensor_tensor(out=t[:, pair, :], in0=hb[i][:, pair, :].bitcast(FP8), in1=hscale[:], op=ALU.mult)
+            else:
+                nc.vector.tensor_tensor(out=hr[i][:], in0=hb[i][:].bitcast(FP8), in1=hscale[:], op=ALU.mult)
 
         def turn_in(i, s, half):
             src = hr[i] if s == 0 else hi[i]
@@ -209,19 +207,40 @@ def tile_wavenetworklm_pb_t_w8_kernel(
                     nc.tensor.transpose(xt[i, s, half][:, jj, u, :], pairs[:, u : K // 2 : 2], ident[:])
 
         def copy_in(i, s, half):
-            t = first(grouped, (i, s), lambda: work.tile([P, NB, T], BF16, name=f"grouped{s}", align_bytes=64))
-            dst = t[:].rearrange("p n t -> p (n t)").bitcast(F32)
+            t = first(grouped, i, lambda: work.tile([P, 2, NB, T], BF16, name="grouped", bufs=5, align_bytes=64))
+            dst = t[:, s].rearrange("p n t -> p (n t)").bitcast(F32)
             nc.scalar.copy(
                 out=dst[:, half * NB : (half + 1) * NB].rearrange("p (j r u) -> p j r u", j=2, u=2),
                 in_=xt[i, s, half][:].rearrange("p j u r -> p j r u"),
             )
+            if i == 0 and s == 1:
+                for j in range(1, 3) if len(scale_copies) == 0 else range(3, J):
+                    scale_copies.append(j)
+                    nc.scalar.copy(out=hscale[:, j, :], in_=hscale[:, 0, :])
 
-        def quantise_h(i, s):
-            hq[i, s] = work.tile([P, NB], U32, name=f"hq{s}", align_bytes=64)
-            hs[i, s] = work.tile([P, NB], U8, name=f"hs{s}", align_bytes=64)
-            nc.vector.quantize_mx(
-                out=hq[i, s][:].bitcast(FP8X4), scales=hs[i, s][:], in_=grouped[i, s][:].rearrange("p n t -> p (n t)")
-            )
+        def h_codes(i):
+            hq[i] = work.tile([P, 2, NB], U32, name="hq", align_bytes=64)
+            hs[i] = work.tile([P, 2, NB], U8, name="hs", align_bytes=64)
+            return hq[i], hs[i]
+
+        def quantise_h(i):
+            if i > 0:
+                codes, planes = h_codes(i)
+                nc.vector.quantize_mx(
+                    out=codes[:].rearrange("p s n -> p (s n)").bitcast(FP8X4),
+                    scales=planes[:].rearrange("p s n -> p (s n)"),
+                    in_=grouped[i][:].rearrange("p s n t -> p (s n t)"),
+                )
+
+        def quantise_h_first(i, s):
+            if i == 0:
+                if i not in hq:
+                    h_codes(i)
+                nc.vector.quantize_mx(
+                    out=hq[i][:, s, :].bitcast(FP8X4),
+                    scales=hs[i][:, s, :],
+                    in_=grouped[i][:, s].rearrange("p n t -> p (n t)"),
+                )
 
         def project(out_ap, i, s, t, toks):
             cols = slice(P * t, P * (t + 1))
@@ -229,8 +248,8 @@ def tile_wavenetworklm_pb_t_w8_kernel(
                 out=out_ap,
                 lhsT=w2p[s][:, cols].bitcast(FP8X4),
                 lhsT_scale=scl2p[4 * s : P, cols],
-                rhs=hq[i, s][:, toks].bitcast(FP8X4),
-                rhs_scale=hs[i, s][:, toks],
+                rhs=hq[i][:, s, toks].bitcast(FP8X4),
+                rhs_scale=hs[i][:, s, toks],
                 start=True,
                 stop=True,
             )
@@ -240,10 +259,12 @@ def tile_wavenetworklm_pb_t_w8_kernel(
             for t in range(T):
                 project(ps[i, "i", j][:, t, :], i, 1, t, slice(P * j, P * (j + 1)))
 
+        def cat_tile(i):
+            return first(catg, i, lambda: work.tile([P, 2, NB, T], BF16, name="catg", bufs=1, align_bytes=64))
+
         def bias_i(i, j):
-            t = first(catg, (i, 1), lambda: work.tile([P, NB, T], BF16, name="catg1", align_bytes=64))
             nc.vector.tensor_tensor(
-                out=t[:, P * j : P * (j + 1), :],
+                out=cat_tile(i)[:, 1, P * j : P * (j + 1), :],
                 in0=ps[i, "i", j][:].rearrange("p t n -> p n t"),
                 in1=bcol[1][:].unsqueeze(1).to_broadcast([P, P, T]),
                 op=ALU.add,
@@ -257,26 +278,23 @@ def tile_wavenetworklm_pb_t_w8_kernel(
             yt = first(y, i, lambda: work.tile([P, T, NB], BF16, name="y", align_bytes=64))
             nc.scalar.activation(out=yt[:, t, :], in_=ps[i, "r", t][:], func=ACT.Identity, bias=bcol[0][:, t : t + 1], scale=1.0)
 
-        def interleave_views(i, toks):
-            t = first(catg, (i, 0), lambda: work.tile([P, NB, T], BF16, name="catg0", align_bytes=64))
-            return (
-                t[:, toks, :].rearrange("p (c i) t -> p c t i", i=4),
-                y[i][:, :, toks].rearrange("p t (c i) -> p c t i", i=4),
+        def interleave(i):
+            nc.gpsimd.tensor_scalar(
+                out=cat_tile(i)[:, 0],
+                in0=y[i][:].rearrange("p t n -> p n t"),
+                scalar1=1.0,
+                scalar2=0.0,
+                op0=ALU.mult,
+                op1=ALU.add,
             )
 
-        def interleave(i):
-            dst, src = interleave_views(i, slice(0, NB - REST))
-            nc.vector.tensor_copy(out=dst, in_=src)
-
-        def interleave_rest(i):
-            dst, src = interleave_views(i, slice(NB - REST, NB))
-            nc.scalar.copy(out=dst, in_=src)
-
-        def quantise_cat(i, s):
-            cq[i, s] = work.tile([P, NB], U32, name=f"cq{s}", align_bytes=64)
-            cs[i, s] = work.tile([P, NB], U8, name=f"cs{s}", align_bytes=64)
+        def quantise_cat(i):
+            cq[i] = work.tile([P, 2, NB], U32, name="cq", align_bytes=64)
+            cs[i] = work.tile([P, 2, NB], U8, name="cs", align_bytes=64)
             nc.vector.quantize_mx(
-                out=cq[i, s][:].bitcast(FP8X4), scales=cs[i, s][:], in_=catg[i, s][:].rearrange("p n t -> p (n t)")
+                out=cq[i][:].rearrange("p s n -> p (s n)").bitcast(FP8X4),
+                scales=cs[i][:].rearrange("p s n -> p (s n)"),
+                in_=catg[i][:].rearrange("p s n t -> p (s n t)"),
             )
 
         def combine(i, c):
@@ -287,8 +305,8 @@ def tile_wavenetworklm_pb_t_w8_kernel(
                     out=ps[i, "e", c][:],
                     lhsT=we[:, s, cols].bitcast(FP8X4),
                     lhsT_scale=scle[4 * s : P, cols],
-                    rhs=cq[i, s][:].bitcast(FP8X4),
-                    rhs_scale=cs[i, s][:],
+                    rhs=cq[i][:, s, :].bitcast(FP8X4),
+                    rhs_scale=cs[i][:, s, :],
                     start=(s == 0),
                     stop=(s == 1),
                 )
@@ -296,14 +314,17 @@ def tile_wavenetworklm_pb_t_w8_kernel(
         def wave_tile(i):
             return first(wt, i, lambda: work.tile([P, T, NB], F32, name="wt"))
 
+        def on_vector(i, c):
+            return (c == 3 and i % 2 == 1) or (c == 1 and i == BLOCKS - 1)
+
         def bias_e(i, c):
-            if i < BLOCKS - 1 or c % 2 == 0:
+            if not on_vector(i, c):
                 nc.scalar.activation(
                     out=wave_tile(i)[:, c, :], in_=ps[i, "e", c][:], func=ACT.Identity, bias=be_col[:, c : c + 1], scale=1.0
                 )
 
-        def bias_e_last(i, c):
-            if i == BLOCKS - 1:
+        def bias_e_vector(i, c):
+            if on_vector(i, c):
                 nc.vector.tensor_scalar(
                     out=wave_tile(i)[:, c, :], in0=ps[i, "e", c][:], scalar1=be_col[:, c : c + 1], scalar2=None, op0=ALU.add
                 )
@@ -334,7 +355,7 @@ def tile_wavenetworklm_pb_t_w8_kernel(
                 inv_sqrt(i, j, j + 1)
 
         def finish(i, j):
-            t = first(res, i, lambda: work.tile([P, J, D], F32, name="res"))
+            t = first(res, i, lambda: work.tile([P, J, D], F32, name="res", bufs=2))
             nc.vector.scalar_tensor_tensor(
                 out=t[:, j, :],
                 in0=turned[i, j][:].rearrange("p c m -> p (c m)"),
@@ -346,10 +367,10 @@ def tile_wavenetworklm_pb_t_w8_kernel(
             nc.sync.dma_start(out=out_dst[i][:, j, :], in_=t[:, j, :])
 
         pieces = {
-            "product": product, "turn_in": turn_in, "copy_in": copy_in, "quantise_h": quantise_h, "project_i": project_i,
-            "bias_i": bias_i, "project_r": project_r, "bias_r": bias_r, "interleave": interleave,
-            "interleave_rest": interleave_rest, "quantise_cat": quantise_cat, "combine": combine, "bias_e": bias_e,
-            "bias_e_last": bias_e_last, "turn_out": turn_out, "square": square, "inv_rms": inv_rms,
+            "product": product, "turn_in": turn_in, "copy_in": copy_in, "quantise_h": quantise_h,
+            "quantise_h_first": quantise_h_first, "project_i": project_i, "bias_i": bias_i, "project_r": project_r,
+            "bias_r": bias_r, "interleave": interleave, "quantise_cat": quantise_cat, "combine": combine, "bias_e": bias_e,
+            "bias_e_vector": bias_e_vector, "turn_out": turn_out, "square": square, "inv_rms": inv_rms,
             "inv_rms_last": inv_rms_last, "finish": finish,
         }
 
@@ -371,7 +392,6 @@ def tile_wavenetworklm_pb_t_w8_kernel(
                 if 0 <= step - lag < BLOCKS:
                     pieces[piece](step - lag, *args)
             if step == 0:
-                nc.scalar.copy(out=hscale[:, 1, :], in_=hscale[:, 0, :])
                 nc.vector.tensor_copy(
                     out=scl2p[:].rearrange("p (t m) -> p m t", t=T), in_=scl2[:].rearrange("p (m t) -> p m t", t=T)
                 )

@@ -23,68 +23,75 @@ D = 512
 NB = 512
 J = NB // P
 BLOCKS = 8
+ROWS = (6, 7)
 
 STEP = [
-    (8, "bias_e", (3,)),
-    (10, "finish", (3,)),
-    (7, "interleave", ()),
-    (9, "turn_out", (2,)),
-    (6, "bias_r", (0,)),
-    (6, "project_r", (1,)),
-    (10, "finish", (2,)),
-    (9, "inv_rms_last", (3,)),
-    (6, "project_i", (2,)),
-    (7, "bias_i", (1,)),
-    (1, "copy_in", (1, 1)),
-    (6, "project_i", (0,)),
-    (4, "copy_in", (0, 1)),
-    (4, "turn_in", (0, 0)),
-    (8, "bias_e_vector", (1,)),
-    (6, "bias_r", (1,)),
-    (7, "bias_i", (3,)),
-    (9, "square", (2,)),
-    (4, "copy_in", (0, 0)),
-    (5, "quantise_h", ()),
-    (9, "inv_rms", (1,)),
-    (9, "finish", (0,)),
-    (9, "finish", (1,)),
-    (5, "quantise_h_first", (0,)),
-    (8, "bias_e_vector", (3,)),
-    (8, "turn_out", (0,)),
-    (1, "turn_in", (1, 0)),
-    (8, "square", (0,)),
-    (1, "copy_in", (1, 0)),
-    (8, "inv_rms_last", (0,)),
-    (7, "quantise_cat", ()),
-    (7, "combine", (2,)),
-    (7, "combine", (1,)),
-    (6, "project_i", (1,)),
-    (8, "turn_out", (1,)),
-    (7, "bias_e", (2,)),
-    (6, "project_i", (3,)),
-    (9, "inv_rms_last", (2,)),
-    (5, "project_r", (2,)),
-    (7, "bias_e", (1,)),
-    (7, "combine", (0,)),
-    (8, "square", (1,)),
-    (8, "turn_out", (3,)),
-    (8, "inv_rms", (0,)),
-    (5, "quantise_h_first", (1,)),
-    (5, "project_r", (3,)),
-    (5, "bias_r", (2,)),
-    (7, "combine", (3,)),
-    (1, "product", ()),
-    (7, "bias_e", (0,)),
-    (5, "project_r", (0,)),
-    (8, "inv_rms_last", (1,)),
-    (6, "bias_i", (2,)),
+    (1, "copy_in", (0, 1)),
+    (3, "bias_i", (1,)),
+    (2, "project_r", (2,)),
+    (4, "bias_e", (3,)),
+    (0, "product", ()),
+    (4, "bias_e", (0,)),
+    (1, "quantise_h_first", (0,)),
+    (2, "bias_r", (2,)),
+    (2, "interleave", ()),
+    (1, "quantise_h_first", (1,)),
+    (5, "inv_rms_last", (1,)),
+    (5, "inv_rms_last", (0,)),
+    (3, "quantise_cat", ()),
+    (3, "combine_rows", (1,)),
+    (2, "project_i", (0,)),
     (0, "turn_in", (1, 1)),
-    (8, "square", (3,)),
-    (6, "bias_i", (0,)),
-    (3, "turn_in", (0, 1)),
-    (5, "bias_r", (3,)),
+    (0, "turn_in", (1, 0)),
+    (5, "turn_out", (2,)),
+    (5, "turn_out", (3,)),
+    (5, "square", (2,)),
+    (2, "project_i", (3,)),
+    (5, "finish", (1,)),
+    (5, "square", (3,)),
+    (3, "combine_rows", (0,)),
+    (5, "finish", (0,)),
+    (0, "copy_in", (1, 1)),
+    (4, "combine", (2,)),
+    (5, "inv_rms", (1,)),
+    (1, "quantise_h", ()),
+    (3, "combine", (1,)),
+    (4, "bias_e", (2,)),
+    (2, "project_i", (2,)),
+    (4, "add_be", (2,)),
+    (1, "project_r", (3,)),
+    (5, "inv_rms_last", (2,)),
+    (2, "bias_i", (0,)),
+    (2, "project_i", (1,)),
+    (0, "copy_in", (1, 0)),
+    (4, "turn_out", (1,)),
+    (4, "add_be", (3,)),
+    (5, "inv_rms_last", (3,)),
+    (4, "turn_out", (0,)),
+    (3, "bias_e", (1,)),
+    (3, "add_be", (1,)),
+    (1, "project_r", (0,)),
+    (1, "bias_r", (3,)),
+    (2, "bias_i", (3,)),
+    (1, "project_r", (1,)),
+    (4, "square", (1,)),
+    (3, "combine_rows", (3,)),
+    (3, "add_be", (0,)),
+    (4, "square", (0,)),
+    (0, "turn_in", (0, 0)),
+    (1, "bias_r", (0,)),
+    (5, "finish", (2,)),
+    (0, "turn_in", (0, 1)),
+    (4, "inv_rms", (0,)),
+    (3, "combine", (3,)),
+    (5, "finish", (3,)),
+    (1, "bias_r", (1,)),
+    (3, "combine_rows", (2,)),
+    (2, "bias_i", (2,)),
+    (0, "copy_in", (0, 0)),
+    (3, "combine", (0,)),
 ]
-LAG = 10
+LAG = 5
 
 
 def tile_wavenetworklm_pb_t_w8_kernel(
@@ -101,8 +108,8 @@ def tile_wavenetworklm_pb_t_w8_kernel(
         loads = ctx.enter_context(tc.tile_pool(name="loads", bufs=BLOCKS))
         work = ctx.enter_context(tc.tile_pool(name="work", bufs=3))
         psum_t = ctx.enter_context(tc.psum_pool(name="psum_t", bufs=2))
-        psum_m = ctx.enter_context(tc.psum_pool(name="psum_m", bufs=3))
-        psum_o = ctx.enter_context(tc.psum_pool(name="psum_o", bufs=3))
+        psum_m = ctx.enter_context(tc.psum_pool(name="psum_m", bufs=4))
+        psum_o = ctx.enter_context(tc.psum_pool(name="psum_o", bufs=2))
         ctx.enter_context(tc.manual_schedule())
 
         ident = keep.tile([P, P], F32, name="ident")
@@ -112,7 +119,9 @@ def tile_wavenetworklm_pb_t_w8_kernel(
         ones_f = keep.tile([P, P], F32, name="ones_f")
         scale_row = keep.tile([P, K], F32, name="scale_row")
         ident_b = keep.tile([P, T], BF16, name="ident_b")
-        rows = keep.tile([P, D], BF16, name="rows")
+        rows = keep.tile([P, 2 * D], BF16, name="rows")
+        still = keep.tile([P, NB], BF16, name="still")
+        be_t = keep.tile([P, D], F32, name="be_t")
         rows4 = keep.tile([P, P], BF16, name="rows4")
         scl2 = keep.tile([P, D], U8, name="scl2", align_bytes=64)
         scle = keep.tile([P, D], U8, name="scle", align_bytes=64)
@@ -125,6 +134,8 @@ def tile_wavenetworklm_pb_t_w8_kernel(
         be_col = keep.tile([P, T], F32, name="be_col")
         g_t = keep.tile([P, D], F32, name="g_t")
 
+        nc.vector.memset(ones[:], 1.0)
+        nc.vector.memset(still[:], 0.0)
         nc.vector.memset(scl2[:].bitcast(I32), 0)
         nc.vector.memset(scle[:].bitcast(I32), 0)
         nc.gpsimd.memset(one_col[:], 1.0)
@@ -133,7 +144,6 @@ def tile_wavenetworklm_pb_t_w8_kernel(
         make_identity(nc, ident[:])
         nc.gpsimd.memset(rows4[:], 0.0)
         nc.gpsimd.memset(rows[:], 0.0)
-        nc.gpsimd.memset(ones[:], 1.0)
         nc.gpsimd.tensor_copy(out=ident_b[:], in_=ident[:, 0:T])
 
         hb = [loads.tile([P, J, K], U8, name="hb", align_bytes=64) for i in range(BLOCKS)]
@@ -146,7 +156,8 @@ def tile_wavenetworklm_pb_t_w8_kernel(
         nc.scalar.dma_start(out=bcol[1][:], in_=b2i.rearrange("(p t) -> p t", t=T))
         nc.scalar.dma_start(out=bcol[0][:], in_=b2r.rearrange("(p t) -> p t", t=T))
         nc.scalar.dma_start(out=rows4[0:T, :], in_=be.rearrange("(c m) -> c m", c=T))
-        nc.scalar.dma_start(out=rows[0:1, :], in_=g_rms.unsqueeze(0))
+        nc.scalar.dma_start(out=rows[0:1, 0:D], in_=be.unsqueeze(0))
+        nc.scalar.dma_start(out=rows[0:1, D : 2 * D], in_=g_rms.unsqueeze(0))
 
         def load_words(s):
             nc.sync.dma_start(out=w2[s][:].bitcast(I32), in_=words[s][0].rearrange("p n t -> p (n t)").bitcast(I32))
@@ -189,7 +200,7 @@ def tile_wavenetworklm_pb_t_w8_kernel(
             return store[key]
 
         def product(i):
-            hr[i] = work.tile([P, J, K], BF16, name="hr", bufs=6, align_bytes=64)
+            hr[i] = work.tile([P, J, K], BF16, name="hr", bufs=3, align_bytes=64)
             if i == 0:
                 for j in range(J):
                     nc.vector.tensor_tensor(
@@ -207,7 +218,7 @@ def tile_wavenetworklm_pb_t_w8_kernel(
                     nc.tensor.transpose(xt[i, s, half][:, jj, u, :], pairs[:, u : K // 2 : 2], ident[:])
 
         def copy_in(i, s, half):
-            t = first(grouped, i, lambda: work.tile([P, 2, NB, T], BF16, name="grouped", bufs=5, align_bytes=64))
+            t = first(grouped, i, lambda: work.tile([P, 2, NB, T], BF16, name="grouped", bufs=2, align_bytes=64))
             dst = t[:, s].rearrange("p n t -> p (n t)").bitcast(F32)
             nc.scalar.copy(
                 out=dst[:, half * NB : (half + 1) * NB].rearrange("p (j r u) -> p j r u", j=2, u=2),
@@ -297,7 +308,29 @@ def tile_wavenetworklm_pb_t_w8_kernel(
                 in_=catg[i][:].rearrange("p s n t -> p (s n t)"),
             )
 
+        def combine_rows(i, j):
+            if i not in ROWS:
+                return
+            ps[i, "w", j] = psum_m.tile([P, D], F32, name="ps")
+            toks = slice(P * j, P * (j + 1))
+            for s in range(2):
+                nc.tensor.matmul_mx(
+                    out=ps[i, "w", j][:],
+                    lhsT=cq[i][:, s, toks].bitcast(FP8X4),
+                    lhsT_scale=cs[i][:, s, toks],
+                    rhs=we[:, s, :].bitcast(FP8X4),
+                    rhs_scale=scle[4 * s : P, :],
+                    start=(s == 0),
+                    stop=(s == 1),
+                )
+
+        def add_be(i, j):
+            if i in ROWS:
+                nc.vector.tensor_tensor(out=wave_tile(i)[:, j, :], in0=ps[i, "w", j][:], in1=be_t[:], op=ALU.add)
+
         def combine(i, c):
+            if i in ROWS:
+                return
             ps[i, "e", c] = psum_m.tile([P, NB], F32, name="ps")
             cols = slice(P * c, P * (c + 1))
             for s in range(2):
@@ -314,31 +347,27 @@ def tile_wavenetworklm_pb_t_w8_kernel(
         def wave_tile(i):
             return first(wt, i, lambda: work.tile([P, T, NB], F32, name="wt"))
 
-        def on_vector(i, c):
-            return (c == 3 and i % 2 == 1) or (c == 1 and i == BLOCKS - 1)
-
         def bias_e(i, c):
-            if not on_vector(i, c):
+            if i not in ROWS:
                 nc.scalar.activation(
                     out=wave_tile(i)[:, c, :], in_=ps[i, "e", c][:], func=ACT.Identity, bias=be_col[:, c : c + 1], scale=1.0
                 )
 
-        def bias_e_vector(i, c):
-            if on_vector(i, c):
-                nc.vector.tensor_scalar(
-                    out=wave_tile(i)[:, c, :], in0=ps[i, "e", c][:], scalar1=be_col[:, c : c + 1], scalar2=None, op0=ALU.add
-                )
-
         def turn_out(i, j):
+            if i in ROWS:
+                return
             turned[i, j] = psum_o.tile([P, T, P], F32, name="turned")
             for c in range(T):
                 nc.tensor.transpose(turned[i, j][:, c, :], wt[i][:, c, P * j : P * (j + 1)], ident[:])
+
+        def waves(i, j):
+            return wt[i][:, j, :] if i in ROWS else turned[i, j][:].rearrange("p c m -> p (c m)")
 
         def square(i, j):
             t = first(rstd, i, lambda: work.tile([P, 2 * J], F32, name="rstd"))
             junk = work.tile([P, D], BF16, name="junk")
             nc.scalar.activation(
-                out=junk[:], in_=turned[i, j][:].rearrange("p c m -> p (c m)"), func=ACT.Square, accum_out=t[:, j : j + 1]
+                out=junk[:], in_=waves(i, j), func=ACT.Square, accum_out=t[:, j : j + 1]
             )
 
         def inv_sqrt(i, a, b):
@@ -358,7 +387,7 @@ def tile_wavenetworklm_pb_t_w8_kernel(
             t = first(res, i, lambda: work.tile([P, J, D], F32, name="res", bufs=2))
             nc.vector.scalar_tensor_tensor(
                 out=t[:, j, :],
-                in0=turned[i, j][:].rearrange("p c m -> p (c m)"),
+                in0=waves(i, j),
                 scalar=rstd[i][:, J + j : J + j + 1],
                 in1=g_t[:],
                 op0=ALU.mult,
@@ -370,9 +399,13 @@ def tile_wavenetworklm_pb_t_w8_kernel(
             "product": product, "turn_in": turn_in, "copy_in": copy_in, "quantise_h": quantise_h,
             "quantise_h_first": quantise_h_first, "project_i": project_i, "bias_i": bias_i, "project_r": project_r,
             "bias_r": bias_r, "interleave": interleave, "quantise_cat": quantise_cat, "combine": combine, "bias_e": bias_e,
-            "bias_e_vector": bias_e_vector, "turn_out": turn_out, "square": square, "inv_rms": inv_rms,
+            "combine_rows": combine_rows, "add_be": add_be, "turn_out": turn_out, "square": square, "inv_rms": inv_rms,
             "inv_rms_last": inv_rms_last, "finish": finish,
         }
+
+        idle_ps = psum_m.tile([P, NB], F32, name="ps")
+        for n in range(3):
+            nc.tensor.matmul(idle_ps[:], ones[:], still[:], start=True, stop=True)
 
         scale_ps = psum_m.tile([P, K], F32, name="ps")
         nc.tensor.matmul(scale_ps[:], ones_f[:], scale_row[:], start=True, stop=True)
@@ -398,6 +431,7 @@ def tile_wavenetworklm_pb_t_w8_kernel(
                 be_ps = psum_m.tile([P, T], F32, name="ps")
                 nc.tensor.matmul(be_ps[:], rows4[:], ident_b[:], start=True, stop=True)
                 nc.scalar.copy(out=be_col[:], in_=be_ps[:])
-                g_ps = psum_m.tile([P, D], F32, name="ps")
-                nc.tensor.matmul(g_ps[:], ones[:], rows[:], start=True, stop=True)
-                nc.scalar.copy(out=g_t[:], in_=g_ps[:])
+                for n, dst in ((1, g_t), (0, be_t)):
+                    row_ps = psum_m.tile([P, D], F32, name="ps")
+                    nc.tensor.matmul(row_ps[:], ones[:], rows[:, n * D : (n + 1) * D], start=True, stop=True)
+                    nc.scalar.copy(out=dst[:], in_=row_ps[:])

from contextlib import ExitStack

import concourse.mybir as mybir
from concourse.masks import make_identity

FLOPS = 2 * 4096 * 512 * 512 * 2 + 2 * 4096 * 1024 * 512
EPS = 1e-6

F32 = mybir.dt.float32
BF16 = mybir.dt.bfloat16
U32 = mybir.dt.uint32
I32 = mybir.dt.int32
U8 = mybir.dt.uint8
FP8 = mybir.dt.float8_e4m3fn
FP8X4 = mybir.dt.float8_e4m3fn_x4
ACT = mybir.ActivationFunctionType
ALU = mybir.AluOpType

P = 128
T = 4
K = 512
D = 512
NB = 512
J = NB // P
BLOCKS = 8
ROWS = (6, 7)

STEP = [
    (1, "copy_in", (0, 1)),
    (3, "bias_i", (1,)),
    (2, "project_r", (2,)),
    (4, "bias_e", (3,)),
    (0, "product", ()),
    (4, "bias_e", (0,)),
    (1, "quantise_h_first", (0,)),
    (2, "bias_r", (2,)),
    (2, "interleave", ()),
    (1, "quantise_h_first", (1,)),
    (5, "inv_rms_last", (1,)),
    (5, "inv_rms_last", (0,)),
    (3, "quantise_cat", ()),
    (3, "combine_rows", (1,)),
    (2, "project_i", (0,)),
    (0, "turn_in", (1, 1)),
    (0, "turn_in", (1, 0)),
    (5, "turn_out", (2,)),
    (5, "turn_out", (3,)),
    (5, "square", (2,)),
    (2, "project_i", (3,)),
    (5, "finish", (1,)),
    (5, "square", (3,)),
    (3, "combine_rows", (0,)),
    (5, "finish", (0,)),
    (0, "copy_in", (1, 1)),
    (4, "combine", (2,)),
    (5, "inv_rms", (1,)),
    (1, "quantise_h", ()),
    (3, "combine", (1,)),
    (4, "bias_e", (2,)),
    (2, "project_i", (2,)),
    (4, "add_be", (2,)),
    (1, "project_r", (3,)),
    (5, "inv_rms_last", (2,)),
    (2, "bias_i", (0,)),
    (2, "project_i", (1,)),
    (0, "copy_in", (1, 0)),
    (4, "turn_out", (1,)),
    (4, "add_be", (3,)),
    (5, "inv_rms_last", (3,)),
    (4, "turn_out", (0,)),
    (3, "bias_e", (1,)),
    (3, "add_be", (1,)),
    (1, "project_r", (0,)),
    (1, "bias_r", (3,)),
    (2, "bias_i", (3,)),
    (1, "project_r", (1,)),
    (4, "square", (1,)),
    (3, "combine_rows", (3,)),
    (3, "add_be", (0,)),
    (4, "square", (0,)),
    (0, "turn_in", (0, 0)),
    (1, "bias_r", (0,)),
    (5, "finish", (2,)),
    (0, "turn_in", (0, 1)),
    (4, "inv_rms", (0,)),
    (3, "combine", (3,)),
    (5, "finish", (3,)),
    (1, "bias_r", (1,)),
    (3, "combine_rows", (2,)),
    (2, "bias_i", (2,)),
    (0, "copy_in", (0, 0)),
    (3, "combine", (0,)),
]
LAG = 5


def tile_wavenetworklm_pb_t_w8_kernel(
    tc, h_r_bytes, h_r_scale, h_i, w2r_words, w2r_scales, b2r, w2i_words, w2i_scales, b2i, We_words, We_scales, be, g_rms, out
):
    nc = tc.nc
    split = "b (h p j) k -> (b h) p j k"
    hr_src = h_r_bytes.rearrange(split, h=2, p=P, j=J)
    hi_src = h_i.rearrange(split, h=2, p=P, j=J)
    out_dst = out.rearrange(split, h=2, p=P, j=J)

    with ExitStack() as ctx:
        keep = ctx.enter_context(tc.tile_pool(name="keep", bufs=1))
        loads = ctx.enter_context(tc.tile_pool(name="loads", bufs=BLOCKS))
        work = ctx.enter_context(tc.tile_pool(name="work", bufs=3))
        psum_t = ctx.enter_context(tc.psum_pool(name="psum_t", bufs=2))
        psum_m = ctx.enter_context(tc.psum_pool(name="psum_m", bufs=4))
        psum_o = ctx.enter_context(tc.psum_pool(name="psum_o", bufs=2))
        ctx.enter_context(tc.manual_schedule())

        ident = keep.tile([P, P], F32, name="ident")
        one_col = keep.tile([P, 1], F32, name="one_col")
        warm = keep.tile([P, 1], F32, name="warm")
        ones = keep.tile([P, P], BF16, name="ones")
        ones_f = keep.tile([P, P], F32, name="ones_f")
        scale_row = keep.tile([P, K], F32, name="scale_row")
        ident_b = keep.tile([P, T], BF16, name="ident_b")
        rows = keep.tile([P, 2 * D], BF16, name="rows")
        still = keep.tile([P, NB], BF16, name="still")
        be_t = keep.tile([P, D], F32, name="be_t")
        rows4 = keep.tile([P, P], BF16, name="rows4")
        scl2 = keep.tile([P, D], U8, name="scl2", align_bytes=64)
        scle = keep.tile([P, D], U8, name="scle", align_bytes=64)
        scl2p = keep.tile([P, D], U8, name="scl2p", align_bytes=64)
        w2 = [keep.tile([P, D], U32, name=f"w2_{s}", align_bytes=64) for s in range(2)]
        w2p = [keep.tile([P, D], U32, name=f"w2p_{s}", align_bytes=64) for s in range(2)]
        we = keep.tile([P, 2, D], U32, name="we", align_bytes=64)
        hscale = keep.tile([P, J, K], F32, name="hscale")
        bcol = [keep.tile([P, T], BF16, name=f"bcol_{s}") for s in range(2)]
        be_col = keep.tile([P, T], F32, name="be_col")
        g_t = keep.tile([P, D], F32, name="g_t")

        nc.vector.memset(ones[:], 1.0)
        nc.vector.memset(still[:], 0.0)
        nc.vector.memset(scl2[:].bitcast(I32), 0)
        nc.vector.memset(scle[:].bitcast(I32), 0)
        nc.gpsimd.memset(one_col[:], 1.0)
        nc.gpsimd.memset(scale_row[:], 0.0)
        nc.gpsimd.memset(ones_f[:], 1.0)
        make_identity(nc, ident[:])
        nc.gpsimd.memset(rows4[:], 0.0)
        nc.gpsimd.memset(rows[:], 0.0)
        nc.gpsimd.tensor_copy(out=ident_b[:], in_=ident[:, 0:T])

        hb = [loads.tile([P, J, K], U8, name="hb", align_bytes=64) for i in range(BLOCKS)]
        hi = [loads.tile([P, J, K], BF16, name="hi", align_bytes=64) for i in range(BLOCKS)]
        words = [w2r_words, w2i_words]
        scales = [w2r_scales, w2i_scales]

        nc.scalar.dma_start(out=scale_row[0:1, :], in_=h_r_scale.rearrange("a b k -> (a b) k"))
        nc.scalar.activation(out=warm[:], in_=one_col[:], func=ACT.Abs_reciprocal_sqrt)
        nc.scalar.dma_start(out=bcol[1][:], in_=b2i.rearrange("(p t) -> p t", t=T))
        nc.scalar.dma_start(out=bcol[0][:], in_=b2r.rearrange("(p t) -> p t", t=T))
        nc.scalar.dma_start(out=rows4[0:T, :], in_=be.rearrange("(c m) -> c m", c=T))
        nc.scalar.dma_start(out=rows[0:1, 0:D], in_=be.unsqueeze(0))
        nc.scalar.dma_start(out=rows[0:1, D : 2 * D], in_=g_rms.unsqueeze(0))

        def load_words(s):
            nc.sync.dma_start(out=w2[s][:].bitcast(I32), in_=words[s][0].rearrange("p n t -> p (n t)").bitcast(I32))

        def load_scales(s):
            for q in range(4):
                nc.sync.dma_start(
                    out=scl2[32 * q + 4 * s : 32 * q + 4 * s + 4, :].bitcast(I32),
                    in_=scales[s][0, 4 * q : 4 * q + 4, :].bitcast(I32),
                )

        nc.sync.dma_start(out=hi[0][:], in_=hi_src[0])
        load_words(1)
        nc.sync.dma_start(out=hb[0][:], in_=hr_src[0])
        load_words(0)
        load_scales(1)
        load_scales(0)
        nc.sync.dma_start(out=hb[1][:], in_=hr_src[1])
        nc.sync.dma_start(out=hi[1][:], in_=hi_src[1])
        nc.sync.dma_start(
            out=we[:].rearrange("p g n -> p g n").bitcast(I32),
            in_=We_words.rearrange("g p n t -> p g (n t)").bitcast(I32),
        )
        for q in range(4):
            nc.sync.dma_start(
                out=scle[32 * q : 32 * q + 8, :].bitcast(I32), in_=We_scales[:, 4 * q : 4 * q + 4, :].bitcast(I32)
            )
        for i in range(2, BLOCKS):
            nc.sync.dma_start(out=hb[i][:], in_=hr_src[i])
            nc.sync.dma_start(out=hi[i][:], in_=hi_src[i])

        hr, hq, hs, y, cq, cs = {}, {}, {}, {}, {}, {}
        grouped, catg, wt, turned, res, rstd, xt, ps = {}, {}, {}, {}, {}, {}, {}, {}

        scale_copies = []

        def first(store, key, make):
            if key not in store:
                store[key] = make()
            return store[key]

        def product(i):
            hr[i] = work.tile([P, J, K], BF16, name="hr", bufs=3, align_bytes=64)
            if i == 0:
                for j in range(J):
                    nc.vector.tensor_tensor(
                        out=hr[i][:, j, :], in0=hb[i][:, j, :].bitcast(FP8), in1=hscale[:, 0, :], op=ALU.mult
                    )
            else:
                nc.vector.tensor_tensor(out=hr[i][:], in0=hb[i][:].bitcast(FP8), in1=hscale[:], op=ALU.mult)

        def turn_in(i, s, half):
            src = hr[i] if s == 0 else hi[i]
            xt[i, s, half] = psum_t.tile([P, 2, 2, P], F32, name="xt")
            for jj in range(2):
                pairs = src[:, 2 * half + jj, :].bitcast(F32)
                for u in range(2):
                    nc.tensor.transpose(xt[i, s, half][:, jj, u, :], pairs[:, u : K // 2 : 2], ident[:])

        def copy_in(i, s, half):
            t = first(grouped, i, lambda: work.tile([P, 2, NB, T], BF16, name="grouped", bufs=2, align_bytes=64))
            dst = t[:, s].rearrange("p n t -> p (n t)").bitcast(F32)
            nc.scalar.copy(
                out=dst[:, half * NB : (half + 1) * NB].rearrange("p (j r u) -> p j r u", j=2, u=2),
                in_=xt[i, s, half][:].rearrange("p j u r -> p j r u"),
            )
            if i == 0 and s == 1:
                for j in range(1, 3) if len(scale_copies) == 0 else range(3, J):
                    scale_copies.append(j)
                    nc.scalar.copy(out=hscale[:, j, :], in_=hscale[:, 0, :])

        def h_codes(i):
            hq[i] = work.tile([P, 2, NB], U32, name="hq", align_bytes=64)
            hs[i] = work.tile([P, 2, NB], U8, name="hs", align_bytes=64)
            return hq[i], hs[i]

        def quantise_h(i):
            if i > 0:
                codes, planes = h_codes(i)
                nc.vector.quantize_mx(
                    out=codes[:].rearrange("p s n -> p (s n)").bitcast(FP8X4),
                    scales=planes[:].rearrange("p s n -> p (s n)"),
                    in_=grouped[i][:].rearrange("p s n t -> p (s n t)"),
                )

        def quantise_h_first(i, s):
            if i == 0:
                if i not in hq:
                    h_codes(i)
                nc.vector.quantize_mx(
                    out=hq[i][:, s, :].bitcast(FP8X4),
                    scales=hs[i][:, s, :],
                    in_=grouped[i][:, s].rearrange("p n t -> p (n t)"),
                )

        def project(out_ap, i, s, t, toks):
            cols = slice(P * t, P * (t + 1))
            nc.tensor.matmul_mx(
                out=out_ap,
                lhsT=w2p[s][:, cols].bitcast(FP8X4),
                lhsT_scale=scl2p[4 * s : P, cols],
                rhs=hq[i][:, s, toks].bitcast(FP8X4),
                rhs_scale=hs[i][:, s, toks],
                start=True,
                stop=True,
            )

        def project_i(i, j):
            ps[i, "i", j] = psum_m.tile([P, T, P], F32, name="ps")
            for t in range(T):
                project(ps[i, "i", j][:, t, :], i, 1, t, slice(P * j, P * (j + 1)))

        def cat_tile(i):
            return first(catg, i, lambda: work.tile([P, 2, NB, T], BF16, name="catg", bufs=1, align_bytes=64))

        def bias_i(i, j):
            nc.vector.tensor_tensor(
                out=cat_tile(i)[:, 1, P * j : P * (j + 1), :],
                in0=ps[i, "i", j][:].rearrange("p t n -> p n t"),
                in1=bcol[1][:].unsqueeze(1).to_broadcast([P, P, T]),
                op=ALU.add,
            )

        def project_r(i, t):
            ps[i, "r", t] = psum_m.tile([P, NB], F32, name="ps")
            project(ps[i, "r", t][:], i, 0, t, slice(0, NB))

        def bias_r(i, t):
            yt = first(y, i, lambda: work.tile([P, T, NB], BF16, name="y", align_bytes=64))
            nc.scalar.activation(out=yt[:, t, :], in_=ps[i, "r", t][:], func=ACT.Identity, bias=bcol[0][:, t : t + 1], scale=1.0)

        def interleave(i):
            nc.gpsimd.tensor_scalar(
                out=cat_tile(i)[:, 0],
                in0=y[i][:].rearrange("p t n -> p n t"),
                scalar1=1.0,
                scalar2=0.0,
                op0=ALU.mult,
                op1=ALU.add,
            )

        def quantise_cat(i):
            cq[i] = work.tile([P, 2, NB], U32, name="cq", align_bytes=64)
            cs[i] = work.tile([P, 2, NB], U8, name="cs", align_bytes=64)
            nc.vector.quantize_mx(
                out=cq[i][:].rearrange("p s n -> p (s n)").bitcast(FP8X4),
                scales=cs[i][:].rearrange("p s n -> p (s n)"),
                in_=catg[i][:].rearrange("p s n t -> p (s n t)"),
            )

        def combine_rows(i, j):
            if i not in ROWS:
                return
            ps[i, "w", j] = psum_m.tile([P, D], F32, name="ps")
            toks = slice(P * j, P * (j + 1))
            for s in range(2):
                nc.tensor.matmul_mx(
                    out=ps[i, "w", j][:],
                    lhsT=cq[i][:, s, toks].bitcast(FP8X4),
                    lhsT_scale=cs[i][:, s, toks],
                    rhs=we[:, s, :].bitcast(FP8X4),
                    rhs_scale=scle[4 * s : P, :],
                    start=(s == 0),
                    stop=(s == 1),
                )

        def add_be(i, j):
            if i in ROWS:
                nc.vector.tensor_tensor(out=wave_tile(i)[:, j, :], in0=ps[i, "w", j][:], in1=be_t[:], op=ALU.add)

        def combine(i, c):
            if i in ROWS:
                return
            ps[i, "e", c] = psum_m.tile([P, NB], F32, name="ps")
            cols = slice(P * c, P * (c + 1))
            for s in range(2):
                nc.tensor.matmul_mx(
                    out=ps[i, "e", c][:],
                    lhsT=we[:, s, cols].bitcast(FP8X4),
                    lhsT_scale=scle[4 * s : P, cols],
                    rhs=cq[i][:, s, :].bitcast(FP8X4),
                    rhs_scale=cs[i][:, s, :],
                    start=(s == 0),
                    stop=(s == 1),
                )

        def wave_tile(i):
            return first(wt, i, lambda: work.tile([P, T, NB], F32, name="wt"))

        def bias_e(i, c):
            if i not in ROWS:
                nc.scalar.activation(
                    out=wave_tile(i)[:, c, :], in_=ps[i, "e", c][:], func=ACT.Identity, bias=be_col[:, c : c + 1], scale=1.0
                )

        def turn_out(i, j):
            if i in ROWS:
                return
            turned[i, j] = psum_o.tile([P, T, P], F32, name="turned")
            for c in range(T):
                nc.tensor.transpose(turned[i, j][:, c, :], wt[i][:, c, P * j : P * (j + 1)], ident[:])

        def waves(i, j):
            return wt[i][:, j, :] if i in ROWS else turned[i, j][:].rearrange("p c m -> p (c m)")

        def square(i, j):
            t = first(rstd, i, lambda: work.tile([P, 2 * J], F32, name="rstd"))
            junk = work.tile([P, D], BF16, name="junk")
            nc.scalar.activation(
                out=junk[:], in_=waves(i, j), func=ACT.Square, accum_out=t[:, j : j + 1]
            )

        def inv_sqrt(i, a, b):
            nc.scalar.activation(
                out=rstd[i][:, J + a : J + b], in_=rstd[i][:, a:b], func=ACT.Abs_reciprocal_sqrt, scale=1.0 / D, bias=EPS
            )

        def inv_rms(i, half):
            if i < BLOCKS - 1:
                inv_sqrt(i, 2 * half, 2 * half + 2)

        def inv_rms_last(i, j):
            if i == BLOCKS - 1:
                inv_sqrt(i, j, j + 1)

        def finish(i, j):
            t = first(res, i, lambda: work.tile([P, J, D], F32, name="res", bufs=2))
            nc.vector.scalar_tensor_tensor(
                out=t[:, j, :],
                in0=waves(i, j),
                scalar=rstd[i][:, J + j : J + j + 1],
                in1=g_t[:],
                op0=ALU.mult,
                op1=ALU.mult,
            )
            nc.sync.dma_start(out=out_dst[i][:, j, :], in_=t[:, j, :])

        pieces = {
            "product": product, "turn_in": turn_in, "copy_in": copy_in, "quantise_h": quantise_h,
            "quantise_h_first": quantise_h_first, "project_i": project_i, "bias_i": bias_i, "project_r": project_r,
            "bias_r": bias_r, "interleave": interleave, "quantise_cat": quantise_cat, "combine": combine, "bias_e": bias_e,
            "combine_rows": combine_rows, "add_be": add_be, "turn_out": turn_out, "square": square, "inv_rms": inv_rms,
            "inv_rms_last": inv_rms_last, "finish": finish,
        }

        idle_ps = psum_m.tile([P, NB], F32, name="ps")
        for n in range(3):
            nc.tensor.matmul(idle_ps[:], ones[:], still[:], start=True, stop=True)

        scale_ps = psum_m.tile([P, K], F32, name="ps")
        nc.tensor.matmul(scale_ps[:], ones_f[:], scale_row[:], start=True, stop=True)

        def permute_words(n):
            nc.vector.tensor_copy(
                out=w2p[n][:].bitcast(I32).rearrange("p (t m) -> p m t", t=T),
                in_=w2[n][:].bitcast(I32).rearrange("p (m t) -> p m t", t=T),
            )

        permute_words(1)
        nc.vector.tensor_copy(out=hscale[:, 0, :], in_=scale_ps[:])
        permute_words(0)

        for step in range(BLOCKS + LAG):
            for lag, piece, args in STEP:
                if 0 <= step - lag < BLOCKS:
                    pieces[piece](step - lag, *args)
            if step == 0:
                nc.vector.tensor_copy(
                    out=scl2p[:].rearrange("p (t m) -> p m t", t=T), in_=scl2[:].rearrange("p (m t) -> p m t", t=T)
                )
                be_ps = psum_m.tile([P, T], F32, name="ps")
                nc.tensor.matmul(be_ps[:], rows4[:], ident_b[:], start=True, stop=True)
                nc.scalar.copy(out=be_col[:], in_=be_ps[:])
                for n, dst in ((1, g_t), (0, be_t)):
                    row_ps = psum_m.tile([P, D], F32, name="ps")
                    nc.tensor.matmul(row_ps[:], ones[:], rows[:, n * D : (n + 1) * D], start=True, stop=True)
                    nc.scalar.copy(out=dst[:], in_=row_ps[:])
